import numpy as np
import ml_dtypes


def mxq(x, axis, fmt="e4m3"):
    dtype, down = {"e4m3": (ml_dtypes.float8_e4m3fn, 7), "e5m2": (ml_dtypes.float8_e5m2, 14)}[fmt]
    v = np.moveaxis(np.asarray(x, np.float32).astype(ml_dtypes.bfloat16).astype(np.float64), axis, -1)
    blocks = v.reshape(v.shape[:-1] + (-1, 32))
    amax = np.abs(blocks).max(-1, keepdims=True)
    byte = np.maximum(np.where(amax > 0, np.frexp(amax)[1] - 1 + 127, 0) - down, 1)
    scale = np.exp2(byte - 127.0)
    codes = (blocks / scale).astype(np.float32).astype(dtype).astype(np.float64)
    return np.moveaxis((codes * scale).reshape(v.shape), -1, axis)


WIDE = False


def mx_kscale(k):
    if not WIDE:
        return np.ones(k)
    levels = np.array([10, -10, 5, -5, 0])
    if k % 512:
        return np.exp2(np.random.permutation(np.resize(levels, k // 32))).repeat(32)
    a = np.empty((k // 512, 16))
    for p in range(k // 512):
        a[p, :8] = np.random.permutation(np.resize(levels, 8))
        for g in range(8):
            far = levels[np.abs(levels - a[p, g]) >= 10]
            a[p, g + 8] = far[np.random.randint(len(far))]
    return np.exp2(a.ravel()).repeat(32)


BF16 = ml_dtypes.bfloat16


def bf(x):
    return np.asarray(x, np.float32).astype(BF16)


def f64(x):
    return np.asarray(x).astype(np.float64)


B, N1, N2, D, H, DH = 4, 1536, 512, 512, 4, 64
E = H * DH


def rope_tables(n, d):
    inv = 1.0 / (10000.0 ** (np.arange(0, d, 2) / d))
    ang = np.outer(np.arange(n), inv)
    return np.repeat(np.cos(ang), 2, axis=-1), np.repeat(np.sin(ang), 2, axis=-1)


def apply_rope(x, cos, sin):
    xr = x.reshape(x.shape[:-1] + (-1, 2))
    x_real, x_imag = xr[..., 0], xr[..., 1]
    x_rot = np.stack([-x_imag, x_real], axis=-1).reshape(x.shape)
    return x * cos[None, None] + x_rot * sin[None, None]


def split_heads(t):
    b, n, _ = t.shape
    return t.reshape(b, n, H, DH).transpose(0, 2, 1, 3)


def setup_inputs():
    s1, s2 = mx_kscale(D), mx_kscale(D)
    cos1, sin1 = rope_tables(N1, DH)
    cos2, sin2 = rope_tables(N2, DH)

    def w(s):
        return bf(np.random.standard_normal((D, E)) * 1.4 / np.sqrt(D) / s[:, None])

    def b():
        return bf(np.random.standard_normal(E) * 0.3)

    return {"x_1": bf(np.random.standard_normal((B, N1, D)) * s1), "x_2": bf(np.random.standard_normal((B, N2, D)) * s2),
            "cos1": bf(cos1), "sin1": bf(sin1), "cos2": bf(cos2), "sin2": bf(sin2),
            "wq1": w(s1), "bq1": b(), "wk1": w(s1), "bk1": b(),
            "wq2": w(s2), "bq2": b(), "wk2": w(s2), "bk2": b()}


def reference(x_1, x_2, cos1, sin1, cos2, sin2, wq1, bq1, wk1, bk1, wq2, bq2, wk2, bk2):
    x1q = mxq(f64(x_1), 2, "e4m3")
    x2q = mxq(f64(x_2), 2, "e4m3")
    q = np.concatenate([(x1q @ mxq(f64(wq1), 0, "e4m3")) + f64(bq1),
                        (x2q @ mxq(f64(wq2), 0, "e4m3")) + f64(bq2)], axis=1)
    k = np.concatenate([(x1q @ mxq(f64(wk1), 0, "e4m3")) + f64(bk1),
                        (x2q @ mxq(f64(wk2), 0, "e4m3")) + f64(bk2)], axis=1)
    q, k = split_heads(q), split_heads(k)
    q = q * (DH ** -0.5)
    cos = np.concatenate([f64(cos1), f64(cos2)], axis=0)
    sin = np.concatenate([f64(sin1), f64(sin2)], axis=0)
    return apply_rope(q, cos, sin), apply_rope(k, cos, sin)

@@ -1,0 +1,268 @@
+from contextlib import ExitStack
+
+import concourse.mybir as mybir
+from concourse.masks import make_identity
+
+F32 = mybir.dt.float32
+BF16 = mybir.dt.bfloat16
+U32 = mybir.dt.uint32
+U8 = mybir.dt.uint8
+FP8X4 = mybir.dt.float8_e4m3fn_x4
+ALU = mybir.AluOpType
+ACT = mybir.ActivationFunctionType
+
+P = 128
+B, N1, N2, D, H, DH = 4, 1536, 512, 512, 4, 64
+E = H * DH
+FLOPS = 2 * B * (N1 + N2) * D * 2 * E
+
+ROUNDS = [(0, tg, b) for tg in range(3) for b in range(B)] + [(1, 0, b) for b in range(B)]
+NR = len(ROUNDS)
+MANUAL = True
+GT = 2
+
+
+def tile_dualmultiheadattention_pa_t_kernel(tc, x_1, x_2, cos1, sin1, cos2, sin2, wq1, bq1, wk1, bk1, wq2, bq2, wk2, bk2, out_0, out_1):
+    nc = tc.nc
+    with ExitStack() as ctx:
+        if MANUAL:
+            ctx.enter_context(tc.manual_schedule())
+        const = ctx.enter_context(tc.tile_pool(name="const", bufs=1))
+        xpool = ctx.enter_context(tc.tile_pool(name="xin", bufs=NR))
+        gpool = ctx.enter_context(tc.tile_pool(name="grouped", bufs=3))
+        cpool = ctx.enter_context(tc.tile_pool(name="codes", bufs=3))
+        tpool = ctx.enter_context(tc.tile_pool(name="proj", bufs=8))
+        rpool = ctx.enter_context(tc.tile_pool(name="prod", bufs=2))
+        ypool = ctx.enter_context(tc.tile_pool(name="res", bufs=3))
+        ps_xt = ctx.enter_context(tc.psum_pool(name="ps_xt", bufs=2))
+        ps_p1 = ctx.enter_context(tc.psum_pool(name="ps_p1", bufs=2))
+        ps_p2 = ctx.enter_context(tc.psum_pool(name="ps_p2", bufs=4))
+
+        def x_view(r):
+            s, tg, b = ROUNDS[r]
+            if s == 0:
+                return x_1[b].rearrange("(p t) k -> p t k", t=12)[:, 4 * tg : 4 * tg + 4, :]
+            return x_2[b].rearrange("(p t) k -> p t k", t=4)
+
+        def out_view(o, r):
+            s, tg, b = ROUNDS[r]
+            if s == 0:
+                return o[b, :, 0:N1, :].rearrange("h (p t) c -> p h t c", t=12)[:, :, 4 * tg : 4 * tg + 4, :]
+            return o[b, :, N1 : N1 + N2, :].rearrange("h (p t) c -> p h t c", t=4)
+
+        xs = []
+
+        def load_x(r):
+            x_sb = xpool.tile([P, 4 * D], BF16, name="x_sb")
+            nc.sync.dma_start(out=x_sb[:].rearrange("p (t k) -> p t k", t=4), in_=x_view(r))
+            xs.append(x_sb)
+
+        ident = const.tile([P, P], F32, name="ident")
+        make_identity(nc, ident[:])
+        brow = const.tile([P, P], BF16, name="brow")
+        nc.vector.memset(brow[:], 0.0)
+
+        wraw = [const.tile([P, 2, 4, E], BF16, name="wraw%d" % s) for s in range(2)]
+        wgrp = [const.tile([P, 2 * E, 4], BF16, name="wgrp%d" % s, align_bytes=64) for s in range(2)]
+        wcod = [const.tile([P, 2 * E], U32, name="wcod%d" % s, align_bytes=64) for s in range(2)]
+        wscl = [const.tile([P, 2 * E], U8, name="wscl%d" % s, align_bytes=64) for s in range(2)]
+        craw = const.tile([P, 16, DH], BF16, name="craw")
+        sraw = const.tile([P, 16, DH], BF16, name="sraw")
+        tab = const.tile([P, 16, 2 * DH], BF16, name="tab")
+
+        def load_w(eng, s, k, w):
+            eng.dma_start(
+                out=wraw[s][:, k].rearrange("q t c -> q (t c)"),
+                in_=w.rearrange("(q t) c -> q (t c)", t=4),
+            )
+
+        load_x(0)
+        load_w(nc.scalar, 0, 0, wq1)
+        load_w(nc.scalar, 0, 1, wk1)
+        for r0, bvec in ((0, bq1), (2, bk1), (4, bq2), (6, bk2)):
+            nc.sync.dma_start(out=brow[r0 : r0 + 2, :], in_=bvec.rearrange("(r m) -> r m", r=2))
+        nc.scalar.dma_start(out=craw[:, 0:12, :], in_=cos1.rearrange("(p t) c -> p t c", t=12))
+        nc.scalar.dma_start(out=sraw[:, 0:12, :], in_=sin1.rearrange("(p t) c -> p t c", t=12))
+        for r in range(1, 6):
+            load_x(r)
+        nc.sync.dma_start(out=craw[:, 12:16, :], in_=cos2.rearrange("(p t) c -> p t c", t=4))
+        nc.sync.dma_start(out=sraw[:, 12:16, :], in_=sin2.rearrange("(p t) c -> p t c", t=4))
+        load_w(nc.sync, 1, 0, wq2)
+        load_w(nc.sync, 1, 1, wk2)
+        for r in range(6, NR):
+            load_x(r)
+
+        def regroup_w(copy, s, k):
+            copy(
+                out=wgrp[s][:, k * E : (k + 1) * E, :].rearrange("p (c i) t -> p c t i", i=4),
+                in_=wraw[s][:, k].rearrange("p t (c i) -> p c t i", i=4),
+            )
+
+        def quantise_w(s):
+            nc.vector.quantize_mx(
+                out=wcod[s][:].bitcast(FP8X4), scales=wscl[s][:], in_=wgrp[s][:].rearrange("p c t -> p (c t)")
+            )
+
+        tabv = tab[:].rearrange("p t (j i e) -> p t j i e", i=2, e=2)
+        crv = craw[:].rearrange("p t (j e) -> p t j e", e=2)
+        srv = sraw[:].rearrange("p t (j e) -> p t j e", e=2)
+
+        def table_op(on_vector, g, k):
+            tsl = slice(4 * g, 4 * g + 4)
+            src, i, e, sign = ((crv, 0, 0, 1.0), (srv, 0, 1, -1.0), (srv, 1, 0, 1.0), (crv, 1, 1, 1.0))[k]
+            dst = tabv[:, tsl, :, i, e]
+            val = src[:, tsl, :, i]
+            if on_vector:
+                nc.vector.tensor_scalar_mul(out=dst, in0=val, scalar1=sign)
+            else:
+                nc.scalar.mul(out=dst, in_=val, mul=sign)
+
+        grouped = {}
+        xcod = {}
+        xscl = {}
+
+        xts = {}
+
+        def transpose_x(r, tau):
+            words = xs[r][:].bitcast(F32)
+            if tau == 0:
+                grp = gpool.tile([P, 8 * P], F32, name="grp", align_bytes=64)
+                grouped[r] = grp
+            half, a = tau // 2, tau % 2
+            if a == 0:
+                xt = ps_xt.tile([P, 2, 2, P], F32, name="xt")
+                xts[r] = xt
+            for u in range(2):
+                nc.tensor.transpose(xts[r][:, a, u, :], words[:, tau * 256 + u : (tau + 1) * 256 : 2], ident[:])
+            if a == 1:
+                nc.scalar.copy(
+                    out=grouped[r][:, half * 512 : (half + 1) * 512].rearrange("q (a p u) -> q a p u", a=2, u=2),
+                    in_=xts[r][:].rearrange("q a u p -> q a p u"),
+                )
+
+        def quantise_x(r):
+            cod = cpool.tile([P, 4 * P], U32, name="xcod", align_bytes=64)
+            scl = cpool.tile([P, 4 * P], U8, name="xscl", align_bytes=64)
+            nc.vector.quantize_mx(out=cod[:].bitcast(FP8X4), scales=scl[:], in_=grouped[r][:].bitcast(BF16))
+            xcod[r] = cod
+            xscl[r] = scl
+
+        proj = {}
+
+        def project(r, fb):
+            s = ROUNDS[r][0]
+            fsl = slice(fb * P, (fb + 1) * P)
+            p1 = ps_p1.tile([P, 4 * P], F32, name="p1")
+            nc.tensor.matmul_mx(
+                out=p1[:],
+                lhsT=wcod[s][:, fsl].bitcast(FP8X4),
+                lhsT_scale=wscl[s][:, fsl],
+                rhs=xcod[r][:].bitcast(FP8X4),
+                rhs_scale=xscl[r][:],
+                start=True,
+                stop=True,
+            )
+            t_sb = tpool.tile([P, 4 * P], F32, name="t_sb")
+            nc.scalar.activation(
+                out=t_sb[:],
+                in_=p1[:],
+                func=ACT.Identity,
+                bias=bias_p[:, 4 * s + fb : 4 * s + fb + 1],
+                scale=(0.125 if fb < 2 else 1.0),
+            )
+            proj[(r, fb)] = t_sb
+
+        regroup_w(nc.vector.tensor_copy, 0, 0)
+        regroup_w(nc.vector.tensor_copy, 0, 1)
+        quantise_w(0)
+        for tau in range(4):
+            transpose_x(0, tau)
+        brow32 = const.tile([P, P], F32, name="brow32")
+        nc.vector.tensor_copy(out=brow32[:], in_=brow[:])
+        bT = ps_p2.tile([P, 4 * P], F32, name="p2")
+        nc.tensor.transpose(bT[:, 0:P], brow32[:], ident[:])
+        quantise_x(0)
+        bias_p = const.tile([P, 8], F32, name="bias_p")
+        bv = bias_p[:].rearrange("p (s k r) -> p s k r", s=2, k=2)
+        tv = bT[:, 0:8].rearrange("p (s k r) -> p s k r", s=2, k=2)
+        nc.vector.tensor_scalar_mul(out=bv[:, :, 0, :], in0=tv[:, :, 0, :], scalar1=0.125)
+        nc.vector.tensor_copy(out=bv[:, :, 1, :], in_=tv[:, :, 1, :])
+        for k in range(4):
+            table_op(True, 0, k)
+        for tau in range(4):
+            transpose_x(1, tau)
+        for fb in range(4):
+            project(0, fb)
+        quantise_x(1)
+        for tau in range(4):
+            transpose_x(2, tau)
+
+        for r in range(NR):
+            s, tg, b = ROUNDS[r]
+            g = tg if s == 0 else 3
+            prod = rpool.tile([P, 4, 8 * P], F32, name="prod")
+            y = ypool.tile([P, 2 * H, 4, DH], F32, name="y")
+            p2s = []
+
+            def back(tau):
+                p2 = ps_p2.tile([P, 4 * P], F32, name="p2")
+                for fb in range(4):
+                    nc.tensor.transpose(
+                        p2[:, fb * P : (fb + 1) * P], proj[(r, fb)][:, tau * P : (tau + 1) * P], ident[:]
+                    )
+                p2s.append(p2)
+
+            def pair_sum(eng, t0, t1):
+                pv = prod[:, t0:t1, :].rearrange("p t (g c e) -> p t g c e", g=8, e=2)
+                eng.tensor_tensor(
+                    out=y[:].rearrange("p g t c -> p t g c")[:, t0:t1],
+                    in0=pv[:, :, :, :, 0],
+                    in1=pv[:, :, :, :, 1],
+                    op=ALU.add,
+                )
+
+            for tau in range(3):
+                back(tau)
+            if r + 1 < NR:
+                for fb in range(4):
+                    project(r + 1, fb)
+            if r + 3 < NR:
+                for tau in range(4):
+                    transpose_x(r + 3, tau)
+            if r < 12:
+                table_op(False, r // 4 + 1, r % 4)
+            if r in (4, 5):
+                regroup_w(nc.scalar.copy, 1, r - 4)
+            for tau in range(3, 4):
+                back(tau)
+            last = r == NR - 1
+            for tau in range(4):
+                nc.vector.tensor_tensor(
+                    out=prod[:, tau, :].rearrange("p (g j i e) -> p g j i e", g=8, i=2, e=2),
+                    in0=p2s[tau][:].rearrange("p (g j e) -> p g j e", g=8, e=2).unsqueeze(3).to_broadcast([P, 8, 32, 2, 2]),
+                    in1=tab[:, 4 * g + tau, :]
+                    .rearrange("p (j i e) -> p j i e", i=2, e=2)
+                    .unsqueeze(1)
+                    .to_broadcast([P, 8, 32, 2, 2]),
+                    op=ALU.mult,
+                )
+                if tau == 1:
+                    if r + 2 < NR:
+                        quantise_x(r + 2)
+                    if r == 7:
+                        quantise_w(1)
+                    pair_sum(nc.gpsimd, 0, 2)
+                    if last:
+                        nc.sync.dma_start(out=out_view(out_0, r)[:, :, 0:2, :], in_=y[:, 0:H, 0:2, :])
+                        nc.sync.dma_start(out=out_view(out_1, r)[:, :, 0:2, :], in_=y[:, H : 2 * H, 0:2, :])
+                if tau == 2 and last:
+                    pair_sum(nc.gpsimd, 2, 3)
+                if tau == 3:
+                    if last:
+                        pair_sum(nc.vector, 3, 4)
+                        nc.sync.dma_start(out=out_view(out_0, r)[:, :, 2:4, :], in_=y[:, 0:H, 2:4, :])
+                        nc.scalar.dma_start(out=out_view(out_1, r)[:, :, 2:4, :], in_=y[:, H : 2 * H, 2:4, :])
+                    else:
+                        pair_sum(nc.gpsimd, 2, 4)
+                        nc.sync.dma_start(out=out_view(out_0, r), in_=y[:, 0:H])
+                        nc.sync.dma_start(out=out_view(out_1, r), in_=y[:, H : 2 * H])

@@ -83,12 +83,13 @@ def tile_dualmultiheadattention_pa_t_kernel(tc, x_1, x_2, cos1, sin1, cos2, sin2
             nc.sync.dma_start(out=brow[r0 : r0 + 2, :], in_=bvec.rearrange("(r m) -> r m", r=2))
         nc.scalar.dma_start(out=craw[:, 0:12, :], in_=cos1.rearrange("(p t) c -> p t c", t=12))
         nc.scalar.dma_start(out=sraw[:, 0:12, :], in_=sin1.rearrange("(p t) c -> p t c", t=12))
-        for r in range(1, 6):
+        load_x(1)
+        load_w(nc.sync, 1, 0, wq2)
+        load_w(nc.sync, 1, 1, wk2)
+        for r in range(2, 6):
             load_x(r)
         nc.sync.dma_start(out=craw[:, 12:16, :], in_=cos2.rearrange("(p t) c -> p t c", t=4))
         nc.sync.dma_start(out=sraw[:, 12:16, :], in_=sin2.rearrange("(p t) c -> p t c", t=4))
-        load_w(nc.sync, 1, 0, wq2)
-        load_w(nc.sync, 1, 1, wk2)
         for r in range(6, NR):
             load_x(r)
 
@@ -194,6 +195,9 @@ def tile_dualmultiheadattention_pa_t_kernel(tc, x_1, x_2, cos1, sin1, cos2, sin2
         for fb in range(4):
             project(0, fb)
         quantise_x(1)
+        regroup_w(nc.vector.tensor_copy, 1, 0)
+        regroup_w(nc.vector.tensor_copy, 1, 1)
+        quantise_w(1)
         for tau in range(4):
             transpose_x(2, tau)
 
@@ -231,8 +235,6 @@ def tile_dualmultiheadattention_pa_t_kernel(tc, x_1, x_2, cos1, sin1, cos2, sin2
                     transpose_x(r + 3, tau)
             if r < 12:
                 table_op(False, r // 4 + 1, r % 4)
-            if r in (4, 5):
-                regroup_w(nc.scalar.copy, 1, r - 4)
             for tau in range(3, 4):
                 back(tau)
             last = r == NR - 1
@@ -249,8 +251,6 @@ def tile_dualmultiheadattention_pa_t_kernel(tc, x_1, x_2, cos1, sin1, cos2, sin2
                 if tau == 1:
                     if r + 2 < NR:
                         quantise_x(r + 2)
-                    if r == 7:
-                        quantise_w(1)
                     pair_sum(nc.gpsimd, 0, 2)
                     if last:
                         nc.sync.dma_start(out=out_view(out_0, r)[:, :, 0:2, :], in_=y[:, 0:H, 0:2, :])

@@ -227,12 +227,13 @@ def tile_dualmultiheadattention_pa_t_kernel(tc, x_1, x_2, cos1, sin1, cos2, sin2
 
             for tau in range(3):
                 back(tau)
-            if r + 1 < NR:
-                for fb in range(4):
-                    project(r + 1, fb)
-            if r + 3 < NR:
-                for tau in range(4):
-                    transpose_x(r + 3, tau)
+            for half in range(2):
+                if r + 1 < NR:
+                    for fb in (2 * half, 2 * half + 1):
+                        project(r + 1, fb)
+                if r + 3 < NR:
+                    for tau in (2 * half, 2 * half + 1):
+                        transpose_x(r + 3, tau)
             if r < 12:
                 table_op(False, r // 4 + 1, r % 4)
             for tau in range(3, 4):

@@ -20,6 +20,8 @@ ROUNDS = [(0, tg, b) for tg in range(3) for b in range(B)] + [(1, 0, b) for b in
 NR = len(ROUNDS)
 MANUAL = True
 GT = 2
+R0 = 4
+ORDER = [("D", 7), ("W", 0, 0), ("X", 0, 0), ("C", 0, 0, 0), ("X", 0, 1), ("C", 0, 1, 0), ("BI",), ("D", 3), ("Q", 0, 0), ("W", 0, 1), ("Q", 0, 1), ("T", 0), ("M", 0, 0, 0), ("M", 0, 1, 0, 1), ("M", 0, 0, 1, 1), ("X", 1, 0), ("C", 1, 0, 0), ("B", 0, 0), ("X", 1, 1), ("C", 1, 1, 0), ("B", 0, 1), ("M", 0, 1, 1), ("W", 1, 0), ("W", 1, 1), ("V", 0, 0), ("Q", 1), ("V", 0, 1), ("S", 0, 0, 1), ("S", 0, 1, 2), ("X", 2, 0), ("C", 2, 0, 0), ("B", 0, 2), ("M", 1, 0), ("B", 0, 3), ("X", 2, 1), ("C", 2, 1, 0), ("M", 1, 1), ("t", 1, 0), ("V", 0, 2), ("V", 0, 3), ("Q", 2), ("S", 0, 2, 4), ("B", 1, 0), ("B", 1, 1), ("B", 1, 2), ("B", 1, 3), ("X", 3, 0), ("C", 3, 0, 0), ("X", 3, 1), ("C", 3, 1, 0), ("M", 2, 0), ("M", 2, 1), ("X", 4, 0), ("C", 4, 0, 0), ("X", 4, 1), ("C", 4, 1, 0), ("t", 1, 1), ("V", 1, 0), ("V", 1, 1), ("S", 1, 0, 1), ("S", 1, 1, 2), ("V", 1, 2), ("V", 1, 3), ("Q", 3), ("S", 1, 2, 4), ("B", 2, 0), ("B", 2, 1), ("B", 2, 2), ("M", 3, 0), ("M", 3, 1), ("X", 5, 0), ("C", 5, 0, 0), ("X", 5, 1), ("C", 5, 1, 0), ("t", 1, 2), ("B", 2, 3), ("V", 2, 0), ("V", 2, 1), ("Q", 4), ("S", 2, 0, 2), ("V", 2, 2), ("V", 2, 3), ("S", 2, 2, 4), ("B", 3, 0), ("B", 3, 1), ("B", 3, 2), ("M", 4, 0), ("M", 4, 1), ("X", 6, 0), ("C", 6, 0, 0), ("X", 6, 1), ("C", 6, 1, 0), ("t", 1, 3), ("B", 3, 3), ("V", 3, 0), ("V", 3, 1), ("Q", 5), ("S", 3, 0, 2), ("V", 3, 2), ("V", 3, 3), ("S", 3, 2, 4)]
 
 
 def tile_dualmultiheadattention_pa_t_kernel(tc, x_1, x_2, cos1, sin1, cos2, sin2, wq1, bq1, wk1, bk1, wq2, bq2, wk2, bk2, out_0, out_1):
@@ -59,6 +61,11 @@ def tile_dualmultiheadattention_pa_t_kernel(tc, x_1, x_2, cos1, sin1, cos2, sin2
 
         ident = const.tile([P, P], F32, name="ident")
         make_identity(nc, ident[:])
+        zeros = const.tile([P, 4 * P], BF16, name="zeros")
+        nc.vector.memset(zeros[:], 0.0)
+        warm = const.tile([P, 1], F32, name="warm")
+        nc.vector.memset(warm[:], 0.0)
+        nc.scalar.activation(out=warm[:], in_=warm[:], func=ACT.Identity, bias=0.0, scale=1.0)
         brow = const.tile([P, P], BF16, name="brow")
         nc.vector.memset(brow[:], 0.0)
 
@@ -76,18 +83,30 @@ def tile_dualmultiheadattention_pa_t_kernel(tc, x_1, x_2, cos1, sin1, cos2, sin2
                 in_=w.rearrange("(q t) c -> q (t c)", t=4),
             )
 
-        load_x(0)
-        load_w(nc.scalar, 0, 0, wq1)
-        load_w(nc.scalar, 0, 1, wk1)
+        def load_tab(g0, g1):
+            for dst, src in ((craw, cos1), (sraw, sin1)):
+                nc.sync.dma_start(
+                    out=dst[:, 4 * g0 : 4 * g1, :],
+                    in_=src.rearrange("(p t) c -> p t c", t=12)[:, 4 * g0 : 4 * g1, :],
+                )
+
+        x0_sb = xpool.tile([P, 4 * D], BF16, name="x_sb")
+        xs.append(x0_sb)
+        for half in range(2):
+            tsl = slice(2 * half, 2 * half + 2)
+            nc.sync.dma_start(out=x0_sb[:].rearrange("p (t k) -> p t k", t=4)[:, tsl, :], in_=x_view(0)[:, tsl, :])
+            load_w(nc.sync, 0, half, (wq1, wk1)[half])
         for r0, bvec in ((0, bq1), (2, bk1), (4, bq2), (6, bk2)):
             nc.sync.dma_start(out=brow[r0 : r0 + 2, :], in_=bvec.rearrange("(r m) -> r m", r=2))
-        nc.scalar.dma_start(out=craw[:, 0:12, :], in_=cos1.rearrange("(p t) c -> p t c", t=12))
-        nc.scalar.dma_start(out=sraw[:, 0:12, :], in_=sin1.rearrange("(p t) c -> p t c", t=12))
         load_x(1)
+        load_tab(0, 1)
         load_w(nc.sync, 1, 0, wq2)
         load_w(nc.sync, 1, 1, wk2)
-        for r in range(2, 6):
-            load_x(r)
+        load_x(2)
+        load_x(3)
+        load_tab(1, 3)
+        load_x(4)
+        load_x(5)
         nc.sync.dma_start(out=craw[:, 12:16, :], in_=cos2.rearrange("(p t) c -> p t c", t=4))
         nc.sync.dma_start(out=sraw[:, 12:16, :], in_=sin2.rearrange("(p t) c -> p t c", t=4))
         for r in range(6, NR):
@@ -99,9 +118,11 @@ def tile_dualmultiheadattention_pa_t_kernel(tc, x_1, x_2, cos1, sin1, cos2, sin2
                 in_=wraw[s][:, k].rearrange("p t (c i) -> p c t i", i=4),
             )
 
-        def quantise_w(s):
+        def quantise_w(s, c0, c1):
             nc.vector.quantize_mx(
-                out=wcod[s][:].bitcast(FP8X4), scales=wscl[s][:], in_=wgrp[s][:].rearrange("p c t -> p (c t)")
+                out=wcod[s][:, c0:c1].bitcast(FP8X4),
+                scales=wscl[s][:, c0:c1],
+                in_=wgrp[s][:, c0:c1, :].rearrange("p c t -> p (c t)"),
             )
 
         tabv = tab[:].rearrange("p t (j i e) -> p t j i e", i=2, e=2)
@@ -136,134 +157,193 @@ def tile_dualmultiheadattention_pa_t_kernel(tc, x_1, x_2, cos1, sin1, cos2, sin2
             for u in range(2):
                 nc.tensor.transpose(xts[r][:, a, u, :], words[:, tau * 256 + u : (tau + 1) * 256 : 2], ident[:])
             if a == 1:
-                nc.scalar.copy(
-                    out=grouped[r][:, half * 512 : (half + 1) * 512].rearrange("q (a p u) -> q a p u", a=2, u=2),
-                    in_=xts[r][:].rearrange("q a u p -> q a p u"),
-                )
+                xts[(r, half)] = xts[r]
 
-        def quantise_x(r):
-            cod = cpool.tile([P, 4 * P], U32, name="xcod", align_bytes=64)
-            scl = cpool.tile([P, 4 * P], U8, name="xscl", align_bytes=64)
-            nc.vector.quantize_mx(out=cod[:].bitcast(FP8X4), scales=scl[:], in_=grouped[r][:].bitcast(BF16))
-            xcod[r] = cod
-            xscl[r] = scl
+        def copy_x(r, half, on_vector):
+            (nc.vector.tensor_copy if on_vector else nc.scalar.copy)(
+                out=grouped[r][:, half * 512 : (half + 1) * 512].rearrange("q (a p u) -> q a p u", a=2, u=2),
+                in_=xts[(r, half)][:].rearrange("q a u p -> q a p u"),
+            )
+
+        def quantise_x(r, half=None):
+            if half in (None, 0):
+                cod = cpool.tile([P, 4 * P], U32, name="xcod", align_bytes=64)
+                scl = cpool.tile([P, 4 * P], U8, name="xscl", align_bytes=64)
+                xcod[r] = cod
+                xscl[r] = scl
+            csl = slice(0, 4 * P) if half is None else slice(2 * P * half, 2 * P * half + 2 * P)
+            nc.vector.quantize_mx(
+                out=xcod[r][:, csl].bitcast(FP8X4),
+                scales=xscl[r][:, csl],
+                in_=grouped[r][:, 2 * csl.start : 2 * csl.stop].bitcast(BF16),
+            )
 
         proj = {}
 
-        def project(r, fb):
+        def project(r, fb, half=None, pool=None):
             s = ROUNDS[r][0]
             fsl = slice(fb * P, (fb + 1) * P)
-            p1 = ps_p1.tile([P, 4 * P], F32, name="p1")
+            if half is None:
+                csl = slice(0, 4 * P)
+            else:
+                csl = slice(2 * P * half, 2 * P * half + 2 * P)
+            n = csl.stop - csl.start
+            if pool is None:
+                p1 = ps_p1.tile([P, 4 * P], F32, name="p1")
+            else:
+                p1 = ps_p2.tile([P, 4 * P], F32, name="p2")
             nc.tensor.matmul_mx(
-                out=p1[:],
+                out=p1[:, 0:n],
                 lhsT=wcod[s][:, fsl].bitcast(FP8X4),
                 lhsT_scale=wscl[s][:, fsl],
-                rhs=xcod[r][:].bitcast(FP8X4),
-                rhs_scale=xscl[r][:],
+                rhs=xcod[r][:, csl].bitcast(FP8X4),
+                rhs_scale=xscl[r][:, csl],
                 start=True,
                 stop=True,
             )
-            t_sb = tpool.tile([P, 4 * P], F32, name="t_sb")
+            if half in (None, 0):
+                t_sb = tpool.tile([P, 4 * P], F32, name="t_sb")
+                proj[(r, fb)] = t_sb
             nc.scalar.activation(
-                out=t_sb[:],
-                in_=p1[:],
+                out=proj[(r, fb)][:, csl],
+                in_=p1[:, 0:n],
                 func=ACT.Identity,
                 bias=bias_p[:, 4 * s + fb : 4 * s + fb + 1],
                 scale=(0.125 if fb < 2 else 1.0),
             )
-            proj[(r, fb)] = t_sb
 
-        regroup_w(nc.vector.tensor_copy, 0, 0)
-        regroup_w(nc.vector.tensor_copy, 0, 1)
-        quantise_w(0)
-        for tau in range(4):
-            transpose_x(0, tau)
-        brow32 = const.tile([P, P], F32, name="brow32")
-        nc.vector.tensor_copy(out=brow32[:], in_=brow[:])
-        bT = ps_p2.tile([P, 4 * P], F32, name="p2")
-        nc.tensor.transpose(bT[:, 0:P], brow32[:], ident[:])
-        quantise_x(0)
-        bias_p = const.tile([P, 8], F32, name="bias_p")
-        bv = bias_p[:].rearrange("p (s k r) -> p s k r", s=2, k=2)
-        tv = bT[:, 0:8].rearrange("p (s k r) -> p s k r", s=2, k=2)
-        nc.vector.tensor_scalar_mul(out=bv[:, :, 0, :], in0=tv[:, :, 0, :], scalar1=0.125)
-        nc.vector.tensor_copy(out=bv[:, :, 1, :], in_=tv[:, :, 1, :])
-        for k in range(4):
-            table_op(True, 0, k)
-        for tau in range(4):
-            transpose_x(1, tau)
-        for fb in range(4):
-            project(0, fb)
-        quantise_x(1)
-        regroup_w(nc.vector.tensor_copy, 1, 0)
-        regroup_w(nc.vector.tensor_copy, 1, 1)
-        quantise_w(1)
-        for tau in range(4):
-            transpose_x(2, tau)
+        def dummies(n):
+            for i in range(n):
+                d = ps_p1.tile([P, 4 * P], F32, name="p1")
+                nc.tensor.matmul(out=d[:], lhsT=zeros[:, 0:P], rhs=zeros[:], start=True, stop=True)
 
-        for r in range(NR):
+        st = {"p2s": {}, "prod": {}, "y": {}}
+
+        def back(r, tau):
+            p2 = ps_p2.tile([P, 4 * P], F32, name="p2")
+            for fb in range(4):
+                nc.tensor.transpose(p2[:, fb * P : (fb + 1) * P], proj[(r, fb)][:, tau * P : (tau + 1) * P], ident[:])
+            st["p2s"][(r, tau)] = p2
+
+        def multiply(r, tau, ks=(0, 1)):
             s, tg, b = ROUNDS[r]
             g = tg if s == 0 else 3
-            prod = rpool.tile([P, 4, 8 * P], F32, name="prod")
-            y = ypool.tile([P, 2 * H, 4, DH], F32, name="y")
-            p2s = []
+            if tau == 0 and ks[0] == 0:
+                prod = rpool.tile([P, 4, 8 * P], F32, name="prod")
+                y = ypool.tile([P, 2 * H, 4, DH], F32, name="y")
+                st["prod"][r] = prod
+                st["y"][r] = y
+            n = 4 * len(ks)
+            c0 = 4 * ks[0]
+            nc.vector.tensor_tensor(
+                out=st["prod"][r][:, tau, P * c0 : P * (c0 + n)].rearrange("p (g j i e) -> p g j i e", g=n, i=2, e=2),
+                in0=st["p2s"][(r, tau)][:, DH * c0 : DH * (c0 + n)]
+                .rearrange("p (g j e) -> p g j e", g=n, e=2)
+                .unsqueeze(3)
+                .to_broadcast([P, n, 32, 2, 2]),
+                in1=tab[:, 4 * g + tau, :]
+                .rearrange("p (j i e) -> p j i e", i=2, e=2)
+                .unsqueeze(1)
+                .to_broadcast([P, n, 32, 2, 2]),
+                op=ALU.mult,
+            )
 
-            def back(tau):
-                p2 = ps_p2.tile([P, 4 * P], F32, name="p2")
-                for fb in range(4):
-                    nc.tensor.transpose(
-                        p2[:, fb * P : (fb + 1) * P], proj[(r, fb)][:, tau * P : (tau + 1) * P], ident[:]
-                    )
-                p2s.append(p2)
+        def pair_sum(eng, r, t0, t1, ks=(0, 1)):
+            gsl = slice(4 * ks[0], 4 * ks[-1] + 4)
+            pv = st["prod"][r][:, t0:t1, :].rearrange("p t (g c e) -> p t g c e", g=8, e=2)[:, :, gsl]
+            eng.tensor_tensor(
+                out=st["y"][r][:].rearrange("p g t c -> p t g c")[:, t0:t1, gsl],
+                in0=pv[:, :, :, :, 0],
+                in1=pv[:, :, :, :, 1],
+                op=ALU.add,
+            )
 
-            def pair_sum(eng, t0, t1):
-                pv = prod[:, t0:t1, :].rearrange("p t (g c e) -> p t g c e", g=8, e=2)
-                eng.tensor_tensor(
-                    out=y[:].rearrange("p g t c -> p t g c")[:, t0:t1],
-                    in0=pv[:, :, :, :, 0],
-                    in1=pv[:, :, :, :, 1],
-                    op=ALU.add,
-                )
+        def store(r, t0=0, t1=4, engine=None):
+            y = st["y"][r]
+            nc.sync.dma_start(out=out_view(out_0, r)[:, :, t0:t1, :], in_=y[:, 0:H, t0:t1, :])
+            (engine or nc.sync).dma_start(out=out_view(out_1, r)[:, :, t0:t1, :], in_=y[:, H : 2 * H, t0:t1, :])
 
-            for tau in range(3):
-                back(tau)
-            for half in range(2):
-                if r + 1 < NR:
-                    for fb in (2 * half, 2 * half + 1):
-                        project(r + 1, fb)
-                if r + 3 < NR:
-                    for tau in (2 * half, 2 * half + 1):
-                        transpose_x(r + 3, tau)
-            if r < 12:
-                table_op(False, r // 4 + 1, r % 4)
-            for tau in range(3, 4):
-                back(tau)
+        bias_p = const.tile([P, 8], F32, name="bias_p")
+
+        def bias():
+            brow32 = const.tile([P, P], F32, name="brow32")
+            nc.vector.tensor_copy(out=brow32[:], in_=brow[:])
+            bT = ps_p2.tile([P, 4 * P], F32, name="p2")
+            nc.tensor.transpose(bT[:, 0:P], brow32[:], ident[:])
+            bv = bias_p[:].rearrange("p (s k r) -> p s k r", s=2, k=2)
+            tv = bT[:, 0:8].rearrange("p (s k r) -> p s k r", s=2, k=2)
+            nc.vector.tensor_scalar_mul(out=bv[:, :, 0, :], in0=tv[:, :, 0, :], scalar1=0.125)
+            nc.vector.tensor_copy(out=bv[:, :, 1, :], in_=tv[:, :, 1, :])
+
+        done_sums = {}
+
+        def run(tok):
+            k = tok[0]
+            if k == "D":
+                dummies(tok[1])
+            elif k == "W":
+                s, kk = tok[1], tok[2]
+                regroup_w(nc.vector.tensor_copy, s, kk)
+                quantise_w(s, kk * E, (kk + 1) * E)
+            elif k == "BI":
+                bias()
+            elif k == "T":
+                for i in range(4):
+                    table_op(tok[1] == 0, tok[1], i)
+            elif k == "t":
+                table_op(False, tok[1], tok[2])
+            elif k == "X":
+                transpose_x(tok[1], 2 * tok[2])
+                transpose_x(tok[1], 2 * tok[2] + 1)
+            elif k == "C":
+                copy_x(tok[1], tok[2], tok[3])
+            elif k == "Q":
+                quantise_x(tok[1], tok[2] if len(tok) > 2 else None)
+            elif k == "M":
+                for fb in (2 * tok[2], 2 * tok[2] + 1):
+                    project(tok[1], fb, tok[3] if len(tok) > 3 else None, ps_p2 if len(tok) > 4 and tok[4] else None)
+            elif k == "B":
+                back(tok[1], tok[2])
+            elif k == "V":
+                multiply(tok[1], tok[2])
+            elif k in ("S", "U"):
+                pair_sum(nc.gpsimd if k == "S" else nc.vector, tok[1], tok[2], tok[3])
+                done_sums[tok[1]] = done_sums.get(tok[1], 0) + tok[3] - tok[2]
+                if done_sums[tok[1]] == 4:
+                    store(tok[1])
+            else:
+                raise AssertionError(tok)
+
+        for tok in ORDER:
+            run(tok)
+        for r in range(R0, NR):
             last = r == NR - 1
+            seq = [("B", r, 0), ("B", r, 1), ("B", r, 2), ("M", r + 1, 0), ("X", r + 3, 0), ("M", r + 1, 1), ("X", r + 3, 1), ("B", r, 3)]
+            if r < 12:
+                seq.append(("t", r // 4 + 1, r % 4))
+            for tok in seq:
+                if tok[0] in "MXB" and tok[1] < NR:
+                    run(tok)
+                    if tok[0] == "X":
+                        run(("C", tok[1], tok[2], 0))
+                elif tok[0] == "t":
+                    run(tok)
+            if last:
+                for k in range(2):
+                    for tau in range(4):
+                        multiply(r, tau, (k,))
+                        if tau == 1:
+                            pair_sum((nc.gpsimd, nc.gpsimd)[k], r, 0, 2, (k,))
+                    pair_sum((nc.gpsimd, nc.vector)[k], r, 2, 4, (k,))
+                    (nc.sync, nc.scalar)[k].dma_start(
+                        out=out_view((out_0, out_1)[k], r), in_=st["y"][r][:, 4 * k : 4 * k + 4]
+                    )
+                continue
             for tau in range(4):
-                nc.vector.tensor_tensor(
-                    out=prod[:, tau, :].rearrange("p (g j i e) -> p g j i e", g=8, i=2, e=2),
-                    in0=p2s[tau][:].rearrange("p (g j e) -> p g j e", g=8, e=2).unsqueeze(3).to_broadcast([P, 8, 32, 2, 2]),
-                    in1=tab[:, 4 * g + tau, :]
-                    .rearrange("p (j i e) -> p j i e", i=2, e=2)
-                    .unsqueeze(1)
-                    .to_broadcast([P, 8, 32, 2, 2]),
-                    op=ALU.mult,
-                )
+                multiply(r, tau)
+                if tau == 1 and r + 2 < NR:
+                    quantise_x(r + 2)
                 if tau == 1:
-                    if r + 2 < NR:
-                        quantise_x(r + 2)
-                    pair_sum(nc.gpsimd, 0, 2)
-                    if last:
-                        nc.sync.dma_start(out=out_view(out_0, r)[:, :, 0:2, :], in_=y[:, 0:H, 0:2, :])
-                        nc.sync.dma_start(out=out_view(out_1, r)[:, :, 0:2, :], in_=y[:, H : 2 * H, 0:2, :])
-                if tau == 2 and last:
-                    pair_sum(nc.gpsimd, 2, 3)
+                    run(("S", r, 0, 2))
                 if tau == 3:
-                    if last:
-                        pair_sum(nc.vector, 3, 4)
-                        nc.sync.dma_start(out=out_view(out_0, r)[:, :, 2:4, :], in_=y[:, 0:H, 2:4, :])
-                        nc.scalar.dma_start(out=out_view(out_1, r)[:, :, 2:4, :], in_=y[:, H : 2 * H, 2:4, :])
-                    else:
-                        pair_sum(nc.gpsimd, 2, 4)
-                        nc.sync.dma_start(out=out_view(out_0, r), in_=y[:, 0:H])
-                        nc.sync.dma_start(out=out_view(out_1, r), in_=y[:, H : 2 * H])
+                    run(("S", r, 2, 4))

@@ -16,19 +16,20 @@ B, N1, N2, D, H, DH = 4, 1536, 512, 512, 4, 64
 E = H * DH
 FLOPS = 2 * B * (N1 + N2) * D * 2 * E
 
+T = 4
+TOKENS = T * P
+PAIRS = DH // 2
+Q, K = 0, 1
+BLOCK = 128
+
 ROUNDS = [(0, tg, b) for tg in range(3) for b in range(B)] + [(1, 0, b) for b in range(B)]
 NR = len(ROUNDS)
-MANUAL = True
-GT = 2
-R0 = 4
-ORDER = [("D", 7), ("W", 0, 0), ("X", 0, 0), ("C", 0, 0, 0), ("X", 0, 1), ("C", 0, 1, 0), ("BI",), ("D", 3), ("Q", 0, 0), ("W", 0, 1), ("Q", 0, 1), ("T", 0), ("M", 0, 0, 0), ("M", 0, 1, 0, 1), ("M", 0, 0, 1, 1), ("X", 1, 0), ("C", 1, 0, 0), ("B", 0, 0), ("X", 1, 1), ("C", 1, 1, 0), ("B", 0, 1), ("M", 0, 1, 1), ("W", 1, 0), ("W", 1, 1), ("V", 0, 0), ("Q", 1), ("V", 0, 1), ("S", 0, 0, 1), ("S", 0, 1, 2), ("X", 2, 0), ("C", 2, 0, 0), ("B", 0, 2), ("M", 1, 0), ("B", 0, 3), ("X", 2, 1), ("C", 2, 1, 0), ("M", 1, 1), ("t", 1, 0), ("V", 0, 2), ("V", 0, 3), ("Q", 2), ("S", 0, 2, 4), ("B", 1, 0), ("B", 1, 1), ("B", 1, 2), ("B", 1, 3), ("X", 3, 0), ("C", 3, 0, 0), ("X", 3, 1), ("C", 3, 1, 0), ("M", 2, 0), ("M", 2, 1), ("X", 4, 0), ("C", 4, 0, 0), ("X", 4, 1), ("C", 4, 1, 0), ("t", 1, 1), ("V", 1, 0), ("V", 1, 1), ("S", 1, 0, 1), ("S", 1, 1, 2), ("V", 1, 2), ("V", 1, 3), ("Q", 3), ("S", 1, 2, 4), ("B", 2, 0), ("B", 2, 1), ("B", 2, 2), ("M", 3, 0), ("M", 3, 1), ("X", 5, 0), ("C", 5, 0, 0), ("X", 5, 1), ("C", 5, 1, 0), ("t", 1, 2), ("B", 2, 3), ("V", 2, 0), ("V", 2, 1), ("Q", 4), ("S", 2, 0, 2), ("V", 2, 2), ("V", 2, 3), ("S", 2, 2, 4), ("B", 3, 0), ("B", 3, 1), ("B", 3, 2), ("M", 4, 0), ("M", 4, 1), ("X", 6, 0), ("C", 6, 0, 0), ("X", 6, 1), ("C", 6, 1, 0), ("t", 1, 3), ("B", 3, 3), ("V", 3, 0), ("V", 3, 1), ("Q", 5), ("S", 3, 0, 2), ("V", 3, 2), ("V", 3, 3), ("S", 3, 2, 4)]
 
 
 def tile_dualmultiheadattention_pa_t_kernel(tc, x_1, x_2, cos1, sin1, cos2, sin2, wq1, bq1, wk1, bk1, wq2, bq2, wk2, bk2, out_0, out_1):
     nc = tc.nc
     with ExitStack() as ctx:
-        if MANUAL:
-            ctx.enter_context(tc.manual_schedule())
+        ctx.enter_context(tc.manual_schedule())
         const = ctx.enter_context(tc.tile_pool(name="const", bufs=1))
         xpool = ctx.enter_context(tc.tile_pool(name="xin", bufs=NR))
         gpool = ctx.enter_context(tc.tile_pool(name="grouped", bufs=3))
@@ -36,36 +37,30 @@ def tile_dualmultiheadattention_pa_t_kernel(tc, x_1, x_2, cos1, sin1, cos2, sin2
         tpool = ctx.enter_context(tc.tile_pool(name="proj", bufs=8))
         rpool = ctx.enter_context(tc.tile_pool(name="prod", bufs=2))
         ypool = ctx.enter_context(tc.tile_pool(name="res", bufs=3))
-        ps_xt = ctx.enter_context(tc.psum_pool(name="ps_xt", bufs=2))
-        ps_p1 = ctx.enter_context(tc.psum_pool(name="ps_p1", bufs=2))
-        ps_p2 = ctx.enter_context(tc.psum_pool(name="ps_p2", bufs=4))
+        ps_x = ctx.enter_context(tc.psum_pool(name="ps_x", bufs=2))
+        ps_proj = ctx.enter_context(tc.psum_pool(name="ps_proj", bufs=2))
+        ps_back = ctx.enter_context(tc.psum_pool(name="ps_back", bufs=4))
 
         def x_view(r):
             s, tg, b = ROUNDS[r]
             if s == 0:
-                return x_1[b].rearrange("(p t) k -> p t k", t=12)[:, 4 * tg : 4 * tg + 4, :]
-            return x_2[b].rearrange("(p t) k -> p t k", t=4)
+                return x_1[b].rearrange("(p t) k -> p t k", t=12)[:, T * tg : T * tg + T, :]
+            return x_2[b].rearrange("(p t) k -> p t k", t=T)
 
-        def out_view(o, r):
+        def out_view(k, r):
             s, tg, b = ROUNDS[r]
+            o = (out_0, out_1)[k]
             if s == 0:
-                return o[b, :, 0:N1, :].rearrange("h (p t) c -> p h t c", t=12)[:, :, 4 * tg : 4 * tg + 4, :]
-            return o[b, :, N1 : N1 + N2, :].rearrange("h (p t) c -> p h t c", t=4)
-
-        xs = []
-
-        def load_x(r):
-            x_sb = xpool.tile([P, 4 * D], BF16, name="x_sb")
-            nc.sync.dma_start(out=x_sb[:].rearrange("p (t k) -> p t k", t=4), in_=x_view(r))
-            xs.append(x_sb)
+                return o[b, :, 0:N1, :].rearrange("h (p t) c -> p h t c", t=12)[:, :, T * tg : T * tg + T, :]
+            return o[b, :, N1 : N1 + N2, :].rearrange("h (p t) c -> p h t c", t=T)
 
         ident = const.tile([P, P], F32, name="ident")
         make_identity(nc, ident[:])
         zeros = const.tile([P, 4 * P], BF16, name="zeros")
         nc.vector.memset(zeros[:], 0.0)
-        warm = const.tile([P, 1], F32, name="warm")
-        nc.vector.memset(warm[:], 0.0)
-        nc.scalar.activation(out=warm[:], in_=warm[:], func=ACT.Identity, bias=0.0, scale=1.0)
+        one_column = const.tile([P, 1], F32, name="one_column")
+        nc.vector.memset(one_column[:], 0.0)
+        nc.scalar.activation(out=one_column[:], in_=one_column[:], func=ACT.Identity, bias=0.0, scale=1.0)
         brow = const.tile([P, P], BF16, name="brow")
         nc.vector.memset(brow[:], 0.0)
 
@@ -76,102 +71,116 @@ def tile_dualmultiheadattention_pa_t_kernel(tc, x_1, x_2, cos1, sin1, cos2, sin2
         craw = const.tile([P, 16, DH], BF16, name="craw")
         sraw = const.tile([P, 16, DH], BF16, name="sraw")
         tab = const.tile([P, 16, 2 * DH], BF16, name="tab")
+        bias_p = const.tile([P, 8], F32, name="bias_p")
 
-        def load_w(eng, s, k, w):
-            eng.dma_start(
-                out=wraw[s][:, k].rearrange("q t c -> q (t c)"),
-                in_=w.rearrange("(q t) c -> q (t c)", t=4),
+        def load_w(s, k, w):
+            nc.sync.dma_start(
+                out=wraw[s][:, k].rearrange("q t c -> q (t c)"), in_=w.rearrange("(q t) c -> q (t c)", t=4)
             )
 
-        def load_tab(g0, g1):
+        def load_angles(g0, g1):
             for dst, src in ((craw, cos1), (sraw, sin1)):
                 nc.sync.dma_start(
-                    out=dst[:, 4 * g0 : 4 * g1, :],
-                    in_=src.rearrange("(p t) c -> p t c", t=12)[:, 4 * g0 : 4 * g1, :],
+                    out=dst[:, T * g0 : T * g1, :],
+                    in_=src.rearrange("(p t) c -> p t c", t=12)[:, T * g0 : T * g1, :],
                 )
 
-        x0_sb = xpool.tile([P, 4 * D], BF16, name="x_sb")
-        xs.append(x0_sb)
+        xs = []
+
+        def new_x():
+            x_sb = xpool.tile([P, T * D], BF16, name="x_sb")
+            xs.append(x_sb)
+            return x_sb[:].rearrange("p (t k) -> p t k", t=T)
+
+        def load_whole_x(r):
+            nc.sync.dma_start(out=new_x(), in_=x_view(r))
+
+        x_first = new_x()
         for half in range(2):
             tsl = slice(2 * half, 2 * half + 2)
-            nc.sync.dma_start(out=x0_sb[:].rearrange("p (t k) -> p t k", t=4)[:, tsl, :], in_=x_view(0)[:, tsl, :])
-            load_w(nc.sync, 0, half, (wq1, wk1)[half])
-        for r0, bvec in ((0, bq1), (2, bk1), (4, bq2), (6, bk2)):
-            nc.sync.dma_start(out=brow[r0 : r0 + 2, :], in_=bvec.rearrange("(r m) -> r m", r=2))
-        load_x(1)
-        load_tab(0, 1)
-        load_w(nc.sync, 1, 0, wq2)
-        load_w(nc.sync, 1, 1, wk2)
-        load_x(2)
-        load_x(3)
-        load_tab(1, 3)
-        load_x(4)
-        load_x(5)
-        nc.sync.dma_start(out=craw[:, 12:16, :], in_=cos2.rearrange("(p t) c -> p t c", t=4))
-        nc.sync.dma_start(out=sraw[:, 12:16, :], in_=sin2.rearrange("(p t) c -> p t c", t=4))
+            nc.sync.dma_start(out=x_first[:, tsl, :], in_=x_view(0)[:, tsl, :])
+            load_w(0, half, (wq1, wk1)[half])
+        for row, bvec in ((0, bq1), (2, bk1), (4, bq2), (6, bk2)):
+            nc.sync.dma_start(out=brow[row : row + 2, :], in_=bvec.rearrange("(r m) -> r m", r=2))
+        load_whole_x(1)
+        load_angles(0, 1)
+        load_w(1, Q, wq2)
+        load_w(1, K, wk2)
+        load_whole_x(2)
+        load_whole_x(3)
+        load_angles(1, 3)
+        load_whole_x(4)
+        load_whole_x(5)
+        nc.sync.dma_start(out=craw[:, 12:16, :], in_=cos2.rearrange("(p t) c -> p t c", t=T))
+        nc.sync.dma_start(out=sraw[:, 12:16, :], in_=sin2.rearrange("(p t) c -> p t c", t=T))
         for r in range(6, NR):
-            load_x(r)
+            load_whole_x(r)
 
-        def regroup_w(copy, s, k):
-            copy(
+        def quantise_w(s, k):
+            nc.vector.tensor_copy(
                 out=wgrp[s][:, k * E : (k + 1) * E, :].rearrange("p (c i) t -> p c t i", i=4),
                 in_=wraw[s][:, k].rearrange("p t (c i) -> p c t i", i=4),
             )
-
-        def quantise_w(s, c0, c1):
+            csl = slice(k * E, (k + 1) * E)
             nc.vector.quantize_mx(
-                out=wcod[s][:, c0:c1].bitcast(FP8X4),
-                scales=wscl[s][:, c0:c1],
-                in_=wgrp[s][:, c0:c1, :].rearrange("p c t -> p (c t)"),
+                out=wcod[s][:, csl].bitcast(FP8X4),
+                scales=wscl[s][:, csl],
+                in_=wgrp[s][:, csl, :].rearrange("p c t -> p (c t)"),
             )
 
-        tabv = tab[:].rearrange("p t (j i e) -> p t j i e", i=2, e=2)
-        crv = craw[:].rearrange("p t (j e) -> p t j e", e=2)
-        srv = sraw[:].rearrange("p t (j e) -> p t j e", e=2)
+        def make_bias_columns():
+            brow32 = const.tile([P, P], F32, name="brow32")
+            nc.vector.tensor_copy(out=brow32[:], in_=brow[:])
+            turned = ps_back.tile([P, 4 * P], F32, name="back")
+            nc.tensor.transpose(turned[:, 0:P], brow32[:], ident[:])
+            cols = bias_p[:].rearrange("p (s k i) -> p s k i", s=2, k=2)
+            vals = turned[:, 0:8].rearrange("p (s k i) -> p s k i", s=2, k=2)
+            nc.vector.tensor_scalar_mul(out=cols[:, :, Q, :], in0=vals[:, :, Q, :], scalar1=DH**-0.5)
+            nc.vector.tensor_copy(out=cols[:, :, K, :], in_=vals[:, :, K, :])
 
-        def table_op(on_vector, g, k):
-            tsl = slice(4 * g, 4 * g + 4)
-            src, i, e, sign = ((crv, 0, 0, 1.0), (srv, 0, 1, -1.0), (srv, 1, 0, 1.0), (crv, 1, 1, 1.0))[k]
-            dst = tabv[:, tsl, :, i, e]
-            val = src[:, tsl, :, i]
-            if on_vector:
-                nc.vector.tensor_scalar_mul(out=dst, in0=val, scalar1=sign)
+        tabv = tab[:].rearrange("p t (j i e) -> p t j i e", i=2, e=2)
+        craw_pairs = craw[:].rearrange("p t (j e) -> p t j e", e=2)
+        sraw_pairs = sraw[:].rearrange("p t (j e) -> p t j e", e=2)
+
+        def table_part(engine_is_vector, g, part):
+            i, e = part // 2, part % 2
+            tsl = slice(T * g, T * g + T)
+            src = (craw_pairs if i == e else sraw_pairs)[:, tsl, :, i]
+            sign = -1.0 if (i, e) == (0, 1) else 1.0
+            if engine_is_vector:
+                nc.vector.tensor_scalar_mul(out=tabv[:, tsl, :, i, e], in0=src, scalar1=sign)
             else:
-                nc.scalar.mul(out=dst, in_=val, mul=sign)
+                nc.scalar.mul(out=tabv[:, tsl, :, i, e], in_=src, mul=sign)
 
         grouped = {}
         xcod = {}
         xscl = {}
 
-        xts = {}
-
-        def transpose_x(r, tau):
+        def turn_x(r, half):
             words = xs[r][:].bitcast(F32)
-            if tau == 0:
-                grp = gpool.tile([P, 8 * P], F32, name="grp", align_bytes=64)
+            if half == 0:
+                grp = gpool.tile([P, 2 * TOKENS], F32, name="grp", align_bytes=64)
                 grouped[r] = grp
-            half, a = tau // 2, tau % 2
-            if a == 0:
-                xt = ps_xt.tile([P, 2, 2, P], F32, name="xt")
-                xts[r] = xt
-            for u in range(2):
-                nc.tensor.transpose(xts[r][:, a, u, :], words[:, tau * 256 + u : (tau + 1) * 256 : 2], ident[:])
-            if a == 1:
-                xts[(r, half)] = xts[r]
-
-        def copy_x(r, half, on_vector):
-            (nc.vector.tensor_copy if on_vector else nc.scalar.copy)(
-                out=grouped[r][:, half * 512 : (half + 1) * 512].rearrange("q (a p u) -> q a p u", a=2, u=2),
-                in_=xts[(r, half)][:].rearrange("q a u p -> q a p u"),
+            xt = ps_x.tile([P, 2, 2, P], F32, name="xt")
+            for a in range(2):
+                t = 2 * half + a
+                for u in range(2):
+                    nc.tensor.transpose(xt[:, a, u, :], words[:, 256 * t + u : 256 * (t + 1) : 2], ident[:])
+            nc.scalar.copy(
+                out=grouped[r][:, half * TOKENS : (half + 1) * TOKENS].rearrange("q (a p u) -> q a p u", a=2, u=2),
+                in_=xt[:].rearrange("q a u p -> q a p u"),
             )
+
+        def columns(half):
+            return slice(0, TOKENS) if half is None else slice(TOKENS // 2 * half, TOKENS // 2 * (half + 1))
 
         def quantise_x(r, half=None):
             if half in (None, 0):
-                cod = cpool.tile([P, 4 * P], U32, name="xcod", align_bytes=64)
-                scl = cpool.tile([P, 4 * P], U8, name="xscl", align_bytes=64)
+                cod = cpool.tile([P, TOKENS], U32, name="xcod", align_bytes=64)
+                scl = cpool.tile([P, TOKENS], U8, name="xscl", align_bytes=64)
                 xcod[r] = cod
                 xscl[r] = scl
-            csl = slice(0, 4 * P) if half is None else slice(2 * P * half, 2 * P * half + 2 * P)
+            csl = columns(half)
             nc.vector.quantize_mx(
                 out=xcod[r][:, csl].bitcast(FP8X4),
                 scales=xscl[r][:, csl],
@@ -180,170 +189,165 @@ def tile_dualmultiheadattention_pa_t_kernel(tc, x_1, x_2, cos1, sin1, cos2, sin2
 
         proj = {}
 
-        def project(r, fb, half=None, pool=None):
+        def project(r, k, half=None, in_back_bank=False):
             s = ROUNDS[r][0]
-            fsl = slice(fb * P, (fb + 1) * P)
-            if half is None:
-                csl = slice(0, 4 * P)
-            else:
-                csl = slice(2 * P * half, 2 * P * half + 2 * P)
+            csl = columns(half)
             n = csl.stop - csl.start
-            if pool is None:
-                p1 = ps_p1.tile([P, 4 * P], F32, name="p1")
-            else:
-                p1 = ps_p2.tile([P, 4 * P], F32, name="p2")
-            nc.tensor.matmul_mx(
-                out=p1[:, 0:n],
-                lhsT=wcod[s][:, fsl].bitcast(FP8X4),
-                lhsT_scale=wscl[s][:, fsl],
-                rhs=xcod[r][:, csl].bitcast(FP8X4),
-                rhs_scale=xscl[r][:, csl],
-                start=True,
-                stop=True,
-            )
-            if half in (None, 0):
-                t_sb = tpool.tile([P, 4 * P], F32, name="t_sb")
-                proj[(r, fb)] = t_sb
-            nc.scalar.activation(
-                out=proj[(r, fb)][:, csl],
-                in_=p1[:, 0:n],
-                func=ACT.Identity,
-                bias=bias_p[:, 4 * s + fb : 4 * s + fb + 1],
-                scale=(0.125 if fb < 2 else 1.0),
-            )
+            for i in range(2):
+                fsl = slice(E * k + BLOCK * i, E * k + BLOCK * (i + 1))
+                if in_back_bank:
+                    acc = ps_back.tile([P, TOKENS], F32, name="back")
+                else:
+                    acc = ps_proj.tile([P, TOKENS], F32, name="acc")
+                nc.tensor.matmul_mx(
+                    out=acc[:, 0:n],
+                    lhsT=wcod[s][:, fsl].bitcast(FP8X4),
+                    lhsT_scale=wscl[s][:, fsl],
+                    rhs=xcod[r][:, csl].bitcast(FP8X4),
+                    rhs_scale=xscl[r][:, csl],
+                    start=True,
+                    stop=True,
+                )
+                if half in (None, 0):
+                    t_sb = tpool.tile([P, TOKENS], F32, name="t_sb")
+                    proj[(r, k, i)] = t_sb
+                col = 4 * s + 2 * k + i
+                nc.scalar.activation(
+                    out=proj[(r, k, i)][:, csl],
+                    in_=acc[:, 0:n],
+                    func=ACT.Identity,
+                    bias=bias_p[:, col : col + 1],
+                    scale=(DH**-0.5 if k == Q else 1.0),
+                )
 
-        def dummies(n):
-            for i in range(n):
-                d = ps_p1.tile([P, 4 * P], F32, name="p1")
-                nc.tensor.matmul(out=d[:], lhsT=zeros[:, 0:P], rhs=zeros[:], start=True, stop=True)
+        backs = {}
 
-        st = {"p2s": {}, "prod": {}, "y": {}}
+        def turn_back(r, t):
+            bank = ps_back.tile([P, 2 * E], F32, name="back")
+            for k in (Q, K):
+                for i in range(2):
+                    c0 = E * k + BLOCK * i
+                    nc.tensor.transpose(bank[:, c0 : c0 + BLOCK], proj[(r, k, i)][:, t * P : (t + 1) * P], ident[:])
+            backs[(r, t)] = bank
 
-        def back(r, tau):
-            p2 = ps_p2.tile([P, 4 * P], F32, name="p2")
-            for fb in range(4):
-                nc.tensor.transpose(p2[:, fb * P : (fb + 1) * P], proj[(r, fb)][:, tau * P : (tau + 1) * P], ident[:])
-            st["p2s"][(r, tau)] = p2
+        prods = {}
+        results = {}
 
-        def multiply(r, tau, ks=(0, 1)):
+        def multiply(r, t, ks=(Q, K)):
             s, tg, b = ROUNDS[r]
-            g = tg if s == 0 else 3
-            if tau == 0 and ks[0] == 0:
-                prod = rpool.tile([P, 4, 8 * P], F32, name="prod")
-                y = ypool.tile([P, 2 * H, 4, DH], F32, name="y")
-                st["prod"][r] = prod
-                st["y"][r] = y
-            n = 4 * len(ks)
-            c0 = 4 * ks[0]
+            row = T * (tg if s == 0 else 3) + t
+            if t == 0 and ks[0] == Q:
+                prod = rpool.tile([P, T, 4 * E], F32, name="prod")
+                y = ypool.tile([P, 2 * H, T, DH], F32, name="y")
+                prods[r] = prod
+                results[r] = y
+            n = H * len(ks)
+            f0 = E * ks[0]
+            shape = [P, n, PAIRS, 2, 2]
             nc.vector.tensor_tensor(
-                out=st["prod"][r][:, tau, P * c0 : P * (c0 + n)].rearrange("p (g j i e) -> p g j i e", g=n, i=2, e=2),
-                in0=st["p2s"][(r, tau)][:, DH * c0 : DH * (c0 + n)]
-                .rearrange("p (g j e) -> p g j e", g=n, e=2)
+                out=prods[r][:, t, 2 * f0 : 2 * (f0 + DH * n)].rearrange("p (h j i e) -> p h j i e", h=n, i=2, e=2),
+                in0=backs[(r, t)][:, f0 : f0 + DH * n]
+                .rearrange("p (h j e) -> p h j e", h=n, e=2)
                 .unsqueeze(3)
-                .to_broadcast([P, n, 32, 2, 2]),
-                in1=tab[:, 4 * g + tau, :]
-                .rearrange("p (j i e) -> p j i e", i=2, e=2)
-                .unsqueeze(1)
-                .to_broadcast([P, n, 32, 2, 2]),
+                .to_broadcast(shape),
+                in1=tab[:, row, :].rearrange("p (j i e) -> p j i e", i=2, e=2).unsqueeze(1).to_broadcast(shape),
                 op=ALU.mult,
             )
 
-        def pair_sum(eng, r, t0, t1, ks=(0, 1)):
-            gsl = slice(4 * ks[0], 4 * ks[-1] + 4)
-            pv = st["prod"][r][:, t0:t1, :].rearrange("p t (g c e) -> p t g c e", g=8, e=2)[:, :, gsl]
-            eng.tensor_tensor(
-                out=st["y"][r][:].rearrange("p g t c -> p t g c")[:, t0:t1, gsl],
-                in0=pv[:, :, :, :, 0],
-                in1=pv[:, :, :, :, 1],
+        def add_pairs(engine, r, t0, t1, ks=(Q, K)):
+            hsl = slice(H * ks[0], H * (ks[-1] + 1))
+            pairs = prods[r][:, t0:t1, :].rearrange("p t (h c e) -> p t h c e", h=2 * H, e=2)[:, :, hsl]
+            engine.tensor_tensor(
+                out=results[r][:].rearrange("p h t c -> p t h c")[:, t0:t1, hsl],
+                in0=pairs[:, :, :, :, 0],
+                in1=pairs[:, :, :, :, 1],
                 op=ALU.add,
             )
 
-        def store(r, t0=0, t1=4, engine=None):
-            y = st["y"][r]
-            nc.sync.dma_start(out=out_view(out_0, r)[:, :, t0:t1, :], in_=y[:, 0:H, t0:t1, :])
-            (engine or nc.sync).dma_start(out=out_view(out_1, r)[:, :, t0:t1, :], in_=y[:, H : 2 * H, t0:t1, :])
+        def store(engine, r, k):
+            engine.dma_start(out=out_view(k, r), in_=results[r][:, H * k : H * (k + 1)])
 
-        bias_p = const.tile([P, 8], F32, name="bias_p")
+        def dummy_passes(n):
+            for i in range(n):
+                acc = ps_proj.tile([P, TOKENS], F32, name="acc")
+                nc.tensor.matmul(out=acc[:], lhsT=zeros[:, 0:P], rhs=zeros[:], start=True, stop=True)
 
-        def bias():
-            brow32 = const.tile([P, P], F32, name="brow32")
-            nc.vector.tensor_copy(out=brow32[:], in_=brow[:])
-            bT = ps_p2.tile([P, 4 * P], F32, name="p2")
-            nc.tensor.transpose(bT[:, 0:P], brow32[:], ident[:])
-            bv = bias_p[:].rearrange("p (s k r) -> p s k r", s=2, k=2)
-            tv = bT[:, 0:8].rearrange("p (s k r) -> p s k r", s=2, k=2)
-            nc.vector.tensor_scalar_mul(out=bv[:, :, 0, :], in0=tv[:, :, 0, :], scalar1=0.125)
-            nc.vector.tensor_copy(out=bv[:, :, 1, :], in_=tv[:, :, 1, :])
+        dummy_passes(6)
+        quantise_w(0, Q)
+        for half in range(2):
+            turn_x(0, half)
+        make_bias_columns()
+        dummy_passes(3)
+        quantise_x(0, 0)
+        quantise_w(0, K)
+        quantise_x(0, 1)
+        for part in range(4):
+            table_part(True, 0, part)
+        project(0, Q, 0)
+        project(0, K, 0, in_back_bank=True)
+        project(0, Q, 1, in_back_bank=True)
+        turn_x(1, 0)
+        turn_back(0, 0)
+        turn_x(1, 1)
+        turn_back(0, 1)
+        project(0, K, 1)
+        for k in (Q, K):
+            quantise_w(1, k)
+        multiply(0, 0)
+        quantise_x(1)
+        multiply(0, 1)
+        add_pairs(nc.gpsimd, 0, 0, 2)
+        turn_x(2, 0)
+        turn_back(0, 2)
+        project(1, Q)
+        turn_back(0, 3)
+        turn_x(2, 1)
+        project(1, K)
+        table_part(False, 1, 0)
+        multiply(0, 2)
+        multiply(0, 3)
+        quantise_x(2)
+        add_pairs(nc.gpsimd, 0, 2, 4)
+        for k in (Q, K):
+            store(nc.sync, 0, k)
 
-        done_sums = {}
-
-        def run(tok):
-            k = tok[0]
-            if k == "D":
-                dummies(tok[1])
-            elif k == "W":
-                s, kk = tok[1], tok[2]
-                regroup_w(nc.vector.tensor_copy, s, kk)
-                quantise_w(s, kk * E, (kk + 1) * E)
-            elif k == "BI":
-                bias()
-            elif k == "T":
-                for i in range(4):
-                    table_op(tok[1] == 0, tok[1], i)
-            elif k == "t":
-                table_op(False, tok[1], tok[2])
-            elif k == "X":
-                transpose_x(tok[1], 2 * tok[2])
-                transpose_x(tok[1], 2 * tok[2] + 1)
-            elif k == "C":
-                copy_x(tok[1], tok[2], tok[3])
-            elif k == "Q":
-                quantise_x(tok[1], tok[2] if len(tok) > 2 else None)
-            elif k == "M":
-                for fb in (2 * tok[2], 2 * tok[2] + 1):
-                    project(tok[1], fb, tok[3] if len(tok) > 3 else None, ps_p2 if len(tok) > 4 and tok[4] else None)
-            elif k == "B":
-                back(tok[1], tok[2])
-            elif k == "V":
-                multiply(tok[1], tok[2])
-            elif k in ("S", "U"):
-                pair_sum(nc.gpsimd if k == "S" else nc.vector, tok[1], tok[2], tok[3])
-                done_sums[tok[1]] = done_sums.get(tok[1], 0) + tok[3] - tok[2]
-                if done_sums[tok[1]] == 4:
-                    store(tok[1])
-            else:
-                raise AssertionError(tok)
-
-        for tok in ORDER:
-            run(tok)
-        for r in range(R0, NR):
-            last = r == NR - 1
-            seq = [("B", r, 0), ("B", r, 1), ("B", r, 2), ("M", r + 1, 0), ("X", r + 3, 0), ("M", r + 1, 1), ("X", r + 3, 1), ("B", r, 3)]
+        for r in range(1, NR):
+            for t in range(3):
+                turn_back(r, t)
+            if r == 1:
+                turn_back(r, 3)
+                turn_x(3, 0)
+            if r + 1 < NR:
+                project(r + 1, Q)
+            if r == 1:
+                turn_x(3, 1)
+            elif r + 3 < NR:
+                turn_x(r + 3, 0)
+            if r + 1 < NR:
+                project(r + 1, K)
+            if r == 1:
+                turn_x(4, 0)
+            if r + 3 < NR:
+                turn_x(r + 3, 1)
             if r < 12:
-                seq.append(("t", r // 4 + 1, r % 4))
-            for tok in seq:
-                if tok[0] in "MXB" and tok[1] < NR:
-                    run(tok)
-                    if tok[0] == "X":
-                        run(("C", tok[1], tok[2], 0))
-                elif tok[0] == "t":
-                    run(tok)
-            if last:
-                for k in range(2):
-                    for tau in range(4):
-                        multiply(r, tau, (k,))
-                        if tau == 1:
-                            pair_sum((nc.gpsimd, nc.gpsimd)[k], r, 0, 2, (k,))
-                    pair_sum((nc.gpsimd, nc.vector)[k], r, 2, 4, (k,))
-                    (nc.sync, nc.scalar)[k].dma_start(
-                        out=out_view((out_0, out_1)[k], r), in_=st["y"][r][:, 4 * k : 4 * k + 4]
-                    )
-                continue
-            for tau in range(4):
-                multiply(r, tau)
-                if tau == 1 and r + 2 < NR:
-                    quantise_x(r + 2)
-                if tau == 1:
-                    run(("S", r, 0, 2))
-                if tau == 3:
-                    run(("S", r, 2, 4))
+                table_part(False, r // 4 + 1, r % 4)
+            if r > 1:
+                turn_back(r, 3)
+
+            if r == NR - 1:
+                for k in (Q, K):
+                    for t in range(T):
+                        multiply(r, t, (k,))
+                        if t == 1:
+                            add_pairs(nc.gpsimd, r, 0, 2, (k,))
+                    add_pairs((nc.gpsimd, nc.vector)[k], r, 2, 4, (k,))
+                    store((nc.sync, nc.scalar)[k], r, k)
+            else:
+                for pair in range(2):
+                    multiply(r, 2 * pair)
+                    multiply(r, 2 * pair + 1)
+                    if r + 2 < NR and pair == (1 if r == 1 else 0):
+                        quantise_x(r + 2)
+                    add_pairs(nc.gpsimd, r, 2 * pair, 2 * pair + 2)
+                for k in (Q, K):
+                    store(nc.sync, r, k)

from contextlib import ExitStack

import concourse.mybir as mybir
from concourse.masks import make_identity

F32 = mybir.dt.float32
BF16 = mybir.dt.bfloat16
U32 = mybir.dt.uint32
U8 = mybir.dt.uint8
FP8X4 = mybir.dt.float8_e4m3fn_x4
ALU = mybir.AluOpType
ACT = mybir.ActivationFunctionType

P = 128
B, N1, N2, D, H, DH = 4, 1536, 512, 512, 4, 64
E = H * DH
FLOPS = 2 * B * (N1 + N2) * D * 2 * E

T = 4
TOKENS = T * P
PAIRS = DH // 2
Q, K = 0, 1
BLOCK = 128

ROUNDS = [(0, tg, b) for tg in range(3) for b in range(B)] + [(1, 0, b) for b in range(B)]
NR = len(ROUNDS)


def tile_dualmultiheadattention_pa_t_kernel(tc, x_1, x_2, cos1, sin1, cos2, sin2, wq1, bq1, wk1, bk1, wq2, bq2, wk2, bk2, out_0, out_1):
    nc = tc.nc
    with ExitStack() as ctx:
        ctx.enter_context(tc.manual_schedule())
        const = ctx.enter_context(tc.tile_pool(name="const", bufs=1))
        xpool = ctx.enter_context(tc.tile_pool(name="xin", bufs=NR))
        gpool = ctx.enter_context(tc.tile_pool(name="grouped", bufs=3))
        cpool = ctx.enter_context(tc.tile_pool(name="codes", bufs=3))
        tpool = ctx.enter_context(tc.tile_pool(name="proj", bufs=8))
        rpool = ctx.enter_context(tc.tile_pool(name="prod", bufs=2))
        ypool = ctx.enter_context(tc.tile_pool(name="res", bufs=3))
        ps_x = ctx.enter_context(tc.psum_pool(name="ps_x", bufs=2))
        ps_proj = ctx.enter_context(tc.psum_pool(name="ps_proj", bufs=2))
        ps_back = ctx.enter_context(tc.psum_pool(name="ps_back", bufs=4))

        def x_view(r):
            s, tg, b = ROUNDS[r]
            if s == 0:
                return x_1[b].rearrange("(p t) k -> p t k", t=12)[:, T * tg : T * tg + T, :]
            return x_2[b].rearrange("(p t) k -> p t k", t=T)

        def out_view(k, r):
            s, tg, b = ROUNDS[r]
            o = (out_0, out_1)[k]
            if s == 0:
                return o[b, :, 0:N1, :].rearrange("h (p t) c -> p h t c", t=12)[:, :, T * tg : T * tg + T, :]
            return o[b, :, N1 : N1 + N2, :].rearrange("h (p t) c -> p h t c", t=T)

        ident = const.tile([P, P], F32, name="ident")
        make_identity(nc, ident[:])
        zeros = const.tile([P, 4 * P], BF16, name="zeros")
        nc.vector.memset(zeros[:], 0.0)
        one_column = const.tile([P, 1], F32, name="one_column")
        nc.vector.memset(one_column[:], 0.0)
        nc.scalar.activation(out=one_column[:], in_=one_column[:], func=ACT.Identity, bias=0.0, scale=1.0)
        brow = const.tile([P, P], BF16, name="brow")
        nc.vector.memset(brow[:], 0.0)

        wraw = [const.tile([P, 2, 4, E], BF16, name="wraw%d" % s) for s in range(2)]
        wgrp = [const.tile([P, 2 * E, 4], BF16, name="wgrp%d" % s, align_bytes=64) for s in range(2)]
        wcod = [const.tile([P, 2 * E], U32, name="wcod%d" % s, align_bytes=64) for s in range(2)]
        wscl = [const.tile([P, 2 * E], U8, name="wscl%d" % s, align_bytes=64) for s in range(2)]
        craw = const.tile([P, 16, DH], BF16, name="craw")
        sraw = const.tile([P, 16, DH], BF16, name="sraw")
        tab = const.tile([P, 16, 2 * DH], BF16, name="tab")
        bias_p = const.tile([P, 8], F32, name="bias_p")

        def load_w(s, k, w):
            nc.sync.dma_start(
                out=wraw[s][:, k].rearrange("q t c -> q (t c)"), in_=w.rearrange("(q t) c -> q (t c)", t=4)
            )

        def load_angles(g0, g1):
            for dst, src in ((craw, cos1), (sraw, sin1)):
                nc.sync.dma_start(
                    out=dst[:, T * g0 : T * g1, :],
                    in_=src.rearrange("(p t) c -> p t c", t=12)[:, T * g0 : T * g1, :],
                )

        xs = []

        def new_x():
            x_sb = xpool.tile([P, T * D], BF16, name="x_sb")
            xs.append(x_sb)
            return x_sb[:].rearrange("p (t k) -> p t k", t=T)

        def load_whole_x(r):
            nc.sync.dma_start(out=new_x(), in_=x_view(r))

        x_first = new_x()
        for half in range(2):
            tsl = slice(2 * half, 2 * half + 2)
            nc.sync.dma_start(out=x_first[:, tsl, :], in_=x_view(0)[:, tsl, :])
            load_w(0, half, (wq1, wk1)[half])
        for row, bvec in ((0, bq1), (2, bk1), (4, bq2), (6, bk2)):
            nc.sync.dma_start(out=brow[row : row + 2, :], in_=bvec.rearrange("(r m) -> r m", r=2))
        load_whole_x(1)
        load_angles(0, 1)
        load_w(1, Q, wq2)
        load_w(1, K, wk2)
        load_whole_x(2)
        load_whole_x(3)
        load_angles(1, 3)
        load_whole_x(4)
        load_whole_x(5)
        nc.sync.dma_start(out=craw[:, 12:16, :], in_=cos2.rearrange("(p t) c -> p t c", t=T))
        nc.sync.dma_start(out=sraw[:, 12:16, :], in_=sin2.rearrange("(p t) c -> p t c", t=T))
        for r in range(6, NR):
            load_whole_x(r)

        def quantise_w(s, k):
            nc.vector.tensor_copy(
                out=wgrp[s][:, k * E : (k + 1) * E, :].rearrange("p (c i) t -> p c t i", i=4),
                in_=wraw[s][:, k].rearrange("p t (c i) -> p c t i", i=4),
            )
            csl = slice(k * E, (k + 1) * E)
            nc.vector.quantize_mx(
                out=wcod[s][:, csl].bitcast(FP8X4),
                scales=wscl[s][:, csl],
                in_=wgrp[s][:, csl, :].rearrange("p c t -> p (c t)"),
            )

        def make_bias_columns():
            brow32 = const.tile([P, P], F32, name="brow32")
            nc.vector.tensor_copy(out=brow32[:], in_=brow[:])
            turned = ps_back.tile([P, 4 * P], F32, name="back")
            nc.tensor.transpose(turned[:, 0:P], brow32[:], ident[:])
            cols = bias_p[:].rearrange("p (s k i) -> p s k i", s=2, k=2)
            vals = turned[:, 0:8].rearrange("p (s k i) -> p s k i", s=2, k=2)
            nc.vector.tensor_scalar_mul(out=cols[:, :, Q, :], in0=vals[:, :, Q, :], scalar1=DH**-0.5)
            nc.vector.tensor_copy(out=cols[:, :, K, :], in_=vals[:, :, K, :])

        tabv = tab[:].rearrange("p t (j i e) -> p t j i e", i=2, e=2)
        craw_pairs = craw[:].rearrange("p t (j e) -> p t j e", e=2)
        sraw_pairs = sraw[:].rearrange("p t (j e) -> p t j e", e=2)

        def table_part(engine_is_vector, g, part):
            i, e = part // 2, part % 2
            tsl = slice(T * g, T * g + T)
            src = (craw_pairs if i == e else sraw_pairs)[:, tsl, :, i]
            sign = -1.0 if (i, e) == (0, 1) else 1.0
            if engine_is_vector:
                nc.vector.tensor_scalar_mul(out=tabv[:, tsl, :, i, e], in0=src, scalar1=sign)
            else:
                nc.scalar.mul(out=tabv[:, tsl, :, i, e], in_=src, mul=sign)

        grouped = {}
        xcod = {}
        xscl = {}

        def turn_x(r, half):
            words = xs[r][:].bitcast(F32)
            if half == 0:
                grp = gpool.tile([P, 2 * TOKENS], F32, name="grp", align_bytes=64)
                grouped[r] = grp
            xt = ps_x.tile([P, 2, 2, P], F32, name="xt")
            for a in range(2):
                t = 2 * half + a
                for u in range(2):
                    nc.tensor.transpose(xt[:, a, u, :], words[:, 256 * t + u : 256 * (t + 1) : 2], ident[:])
            nc.scalar.copy(
                out=grouped[r][:, half * TOKENS : (half + 1) * TOKENS].rearrange("q (a p u) -> q a p u", a=2, u=2),
                in_=xt[:].rearrange("q a u p -> q a p u"),
            )

        def columns(half):
            return slice(0, TOKENS) if half is None else slice(TOKENS // 2 * half, TOKENS // 2 * (half + 1))

        def quantise_x(r, half=None):
            if half in (None, 0):
                cod = cpool.tile([P, TOKENS], U32, name="xcod", align_bytes=64)
                scl = cpool.tile([P, TOKENS], U8, name="xscl", align_bytes=64)
                xcod[r] = cod
                xscl[r] = scl
            csl = columns(half)
            nc.vector.quantize_mx(
                out=xcod[r][:, csl].bitcast(FP8X4),
                scales=xscl[r][:, csl],
                in_=grouped[r][:, 2 * csl.start : 2 * csl.stop].bitcast(BF16),
            )

        proj = {}

        def project(r, k, half=None, in_back_bank=False):
            s = ROUNDS[r][0]
            csl = columns(half)
            n = csl.stop - csl.start
            for i in range(2):
                fsl = slice(E * k + BLOCK * i, E * k + BLOCK * (i + 1))
                if in_back_bank:
                    acc = ps_back.tile([P, TOKENS], F32, name="back")
                else:
                    acc = ps_proj.tile([P, TOKENS], F32, name="acc")
                nc.tensor.matmul_mx(
                    out=acc[:, 0:n],
                    lhsT=wcod[s][:, fsl].bitcast(FP8X4),
                    lhsT_scale=wscl[s][:, fsl],
                    rhs=xcod[r][:, csl].bitcast(FP8X4),
                    rhs_scale=xscl[r][:, csl],
                    start=True,
                    stop=True,
                )
                if half in (None, 0):
                    t_sb = tpool.tile([P, TOKENS], F32, name="t_sb")
                    proj[(r, k, i)] = t_sb
                col = 4 * s + 2 * k + i
                nc.scalar.activation(
                    out=proj[(r, k, i)][:, csl],
                    in_=acc[:, 0:n],
                    func=ACT.Identity,
                    bias=bias_p[:, col : col + 1],
                    scale=(DH**-0.5 if k == Q else 1.0),
                )

        backs = {}

        def turn_back(r, t):
            bank = ps_back.tile([P, 2 * E], F32, name="back")
            for k in (Q, K):
                for i in range(2):
                    c0 = E * k + BLOCK * i
                    nc.tensor.transpose(bank[:, c0 : c0 + BLOCK], proj[(r, k, i)][:, t * P : (t + 1) * P], ident[:])
            backs[(r, t)] = bank

        prods = {}
        results = {}

        def multiply(r, t, ks=(Q, K)):
            s, tg, b = ROUNDS[r]
            row = T * (tg if s == 0 else 3) + t
            if t == 0 and ks[0] == Q:
                prod = rpool.tile([P, T, 4 * E], F32, name="prod")
                y = ypool.tile([P, 2 * H, T, DH], F32, name="y")
                prods[r] = prod
                results[r] = y
            n = H * len(ks)
            f0 = E * ks[0]
            shape = [P, n, PAIRS, 2, 2]
            nc.vector.tensor_tensor(
                out=prods[r][:, t, 2 * f0 : 2 * (f0 + DH * n)].rearrange("p (h j i e) -> p h j i e", h=n, i=2, e=2),
                in0=backs[(r, t)][:, f0 : f0 + DH * n]
                .rearrange("p (h j e) -> p h j e", h=n, e=2)
                .unsqueeze(3)
                .to_broadcast(shape),
                in1=tab[:, row, :].rearrange("p (j i e) -> p j i e", i=2, e=2).unsqueeze(1).to_broadcast(shape),
                op=ALU.mult,
            )

        def add_pairs(engine, r, t0, t1, ks=(Q, K)):
            hsl = slice(H * ks[0], H * (ks[-1] + 1))
            pairs = prods[r][:, t0:t1, :].rearrange("p t (h c e) -> p t h c e", h=2 * H, e=2)[:, :, hsl]
            engine.tensor_tensor(
                out=results[r][:].rearrange("p h t c -> p t h c")[:, t0:t1, hsl],
                in0=pairs[:, :, :, :, 0],
                in1=pairs[:, :, :, :, 1],
                op=ALU.add,
            )

        def store(engine, r, k):
            engine.dma_start(out=out_view(k, r), in_=results[r][:, H * k : H * (k + 1)])

        def dummy_passes(n):
            for i in range(n):
                acc = ps_proj.tile([P, TOKENS], F32, name="acc")
                nc.tensor.matmul(out=acc[:], lhsT=zeros[:, 0:P], rhs=zeros[:], start=True, stop=True)

        dummy_passes(6)
        quantise_w(0, Q)
        for half in range(2):
            turn_x(0, half)
        make_bias_columns()
        dummy_passes(3)
        quantise_x(0, 0)
        quantise_w(0, K)
        quantise_x(0, 1)
        for part in range(4):
            table_part(True, 0, part)
        project(0, Q, 0)
        project(0, K, 0, in_back_bank=True)
        project(0, Q, 1, in_back_bank=True)
        turn_x(1, 0)
        turn_back(0, 0)
        turn_x(1, 1)
        turn_back(0, 1)
        project(0, K, 1)
        for k in (Q, K):
            quantise_w(1, k)
        multiply(0, 0)
        quantise_x(1)
        multiply(0, 1)
        add_pairs(nc.gpsimd, 0, 0, 2)
        turn_x(2, 0)
        turn_back(0, 2)
        project(1, Q)
        turn_back(0, 3)
        turn_x(2, 1)
        project(1, K)
        table_part(False, 1, 0)
        multiply(0, 2)
        multiply(0, 3)
        quantise_x(2)
        add_pairs(nc.gpsimd, 0, 2, 4)
        for k in (Q, K):
            store(nc.sync, 0, k)

        for r in range(1, NR):
            for t in range(3):
                turn_back(r, t)
            if r == 1:
                turn_back(r, 3)
                turn_x(3, 0)
            if r + 1 < NR:
                project(r + 1, Q)
            if r == 1:
                turn_x(3, 1)
            elif r + 3 < NR:
                turn_x(r + 3, 0)
            if r + 1 < NR:
                project(r + 1, K)
            if r == 1:
                turn_x(4, 0)
            if r + 3 < NR:
                turn_x(r + 3, 1)
            if r < 12:
                table_part(False, r // 4 + 1, r % 4)
            if r > 1:
                turn_back(r, 3)

            if r == NR - 1:
                for k in (Q, K):
                    for t in range(T):
                        multiply(r, t, (k,))
                        if t == 1:
                            add_pairs(nc.gpsimd, r, 0, 2, (k,))
                    add_pairs((nc.gpsimd, nc.vector)[k], r, 2, 4, (k,))
                    store((nc.sync, nc.scalar)[k], r, k)
            else:
                for pair in range(2):
                    multiply(r, 2 * pair)
                    multiply(r, 2 * pair + 1)
                    if r + 2 < NR and pair == (1 if r == 1 else 0):
                        quantise_x(r + 2)
                    add_pairs(nc.gpsimd, r, 2 * pair, 2 * pair + 2)
                for k in (Q, K):
                    store(nc.sync, r, k)
